import numpy as np
import ml_dtypes


def mxq(x, axis, fmt="e4m3"):
    dtype, down = {"e4m3": (ml_dtypes.float8_e4m3fn, 7), "e5m2": (ml_dtypes.float8_e5m2, 14)}[fmt]
    v = np.moveaxis(np.asarray(x, np.float32).astype(ml_dtypes.bfloat16).astype(np.float64), axis, -1)
    blocks = v.reshape(v.shape[:-1] + (-1, 32))
    amax = np.abs(blocks).max(-1, keepdims=True)
    byte = np.maximum(np.where(amax > 0, np.frexp(amax)[1] - 1 + 127, 0) - down, 1)
    scale = np.exp2(byte - 127.0)
    codes = (blocks / scale).astype(np.float32).astype(dtype).astype(np.float64)
    return np.moveaxis((codes * scale).reshape(v.shape), -1, axis)


WIDE = False


def mx_kscale(k):
    if not WIDE:
        return np.ones(k)
    levels = np.array([10, -10, 5, -5, 0])
    if k % 512:
        return np.exp2(np.random.permutation(np.resize(levels, k // 32))).repeat(32)
    a = np.empty((k // 512, 16))
    for p in range(k // 512):
        a[p, :8] = np.random.permutation(np.resize(levels, 8))
        for g in range(8):
            far = levels[np.abs(levels - a[p, g]) >= 10]
            a[p, g + 8] = far[np.random.randint(len(far))]
    return np.exp2(a.ravel()).repeat(32)


BF16 = ml_dtypes.bfloat16


def bf(x):
    return np.asarray(x, np.float32).astype(BF16)


def f64(x):
    return np.asarray(x).astype(np.float64)


B, N, G, L = 1024, 512, 128, 768
N2 = 2 * N


def setup_inputs():
    s = mx_kscale(N2)
    return {
        "Volt": bf(np.random.standard_normal((B, N2)) * s),
        "Y": bf(np.random.standard_normal((N2, N2)) / np.sqrt(N2) / s[None, :] / s[:, None]),
        "Yconj": bf(np.random.standard_normal((N2, N2)) / np.sqrt(N2) / s[None, :] / s[:, None]),
    }


def reference(Volt, Y, Yconj):
    v = f64(Volt)
    vq = mxq(v, 1, "e4m3")
    quad_p = v * (vq @ mxq(f64(Y), 1, "e4m3").T)
    quad_q = v * (vq @ mxq(f64(Yconj), 1, "e4m3").T)
    return quad_p, quad_q

@@ -1,0 +1,243 @@
+from contextlib import ExitStack
+
+import concourse.mybir as mybir
+from concourse.masks import make_identity
+
+F32 = mybir.dt.float32
+BF16 = mybir.dt.bfloat16
+U32 = mybir.dt.uint32
+U8 = mybir.dt.uint8
+FP8X4 = mybir.dt.float8_e4m3fn_x4
+MULT = mybir.AluOpType.mult
+
+P = 128
+K = 1024
+KW = K // 2
+FLOPS = 2 * 2 * 1024 * 1024 * 1024
+
+OFFLOAD = ((1, 0, 0), (1, 2, 0), (1, 4, 0), (1, 6, 0))
+
+
+def tile_pinnlayer_pb_kernel(tc, Volt, Y, Yconj, out_0, out_1):
+    nc = tc.nc
+    mats = (Y, Yconj)
+    out_views = tuple(o.rearrange("(p t) r -> p t r", t=8) for o in (out_0, out_1))
+    volt_view = Volt.rearrange("(p t) k -> p t k", t=8)
+
+    with ExitStack() as ctx:
+        keep = ctx.enter_context(tc.tile_pool(name="keep", bufs=1))
+        tp_pool = ctx.enter_context(tc.psum_pool(name="tp", bufs=4))
+        acc_pool = ctx.enter_context(tc.psum_pool(name="acc", bufs=4))
+        ctx.enter_context(tc.manual_schedule())
+
+        ident = keep.tile([P, P], F32, name="ident")
+        make_identity(nc, ident[:])
+        zeros = keep.tile([P, 512], BF16, name="zeros")
+        nc.vector.memset(zeros[:], 0.0)
+
+        def warm(count):
+            for n in range(count):
+                w = acc_pool.tile([P, 512], F32, tag="acc", name="warm")
+                nc.tensor.matmul(out=w[:], lhsT=zeros[:, 0:P], rhs=zeros[:], start=True, stop=True)
+
+        def load(view, rows, name):
+            raw = keep.tile([P, rows * K], BF16, name=name)
+            nc.sync.dma_start(out=raw[:].rearrange("p (t k) -> p t k", t=rows), in_=view)
+            return raw
+
+        def load_half(m, h, pieces):
+            view = mats[m][512 * h : 512 * (h + 1), :].rearrange("(q t) k -> q t k", t=4)
+            per = 4 // pieces
+            chunks = []
+            for s in range(pieces):
+                raw = load(view[:, per * s : per * (s + 1), :], per, "yraw%d%d%d" % (m, h, s))
+                words = raw[:].bitcast(F32)
+                for t in range(per):
+                    chunks.append(words[:, KW * t : KW * (t + 1)])
+            return chunks
+
+        y_chunks = {}
+        v_raw = []
+        y_chunks[(0, 0)] = load_half(0, 0, 2)
+        for j in range(4):
+            v_raw.append(load(volt_view[:, 2 * j : 2 * j + 2, :], 2, "vraw%d" % j))
+        y_chunks[(0, 1)] = load_half(0, 1, 1)
+        y_chunks[(1, 0)] = load_half(1, 0, 1)
+        y_chunks[(1, 1)] = load_half(1, 1, 1)
+
+        y_grp = {}
+        y_codes = {}
+        y_scales = {}
+        for m in range(2):
+            for h in range(2):
+                if (m, h) == (0, 0):
+                    for t in range(4):
+                        y_grp[(m, h, t)] = keep.tile([P, 1024], BF16, name="ygrp%d%d%d" % (m, h, t), align_bytes=64)
+                else:
+                    y_grp[(m, h)] = keep.tile([P, 4096], BF16, name="ygrp%d%d" % (m, h), align_bytes=64)
+                y_codes[(m, h)] = keep.tile([P, 1024], U32, name="ycod%d%d" % (m, h), align_bytes=64)
+                y_scales[(m, h)] = keep.tile([P, 1024], U8, name="yscl%d%d" % (m, h), align_bytes=64)
+        v_grp = {}
+        v_codes = []
+        v_scales = []
+        o_sb = {}
+        for i in range(4):
+            v_grp[i] = keep.tile([P, 1024], BF16, name="vgrpc%d" % i, align_bytes=64)
+        for j in range(4):
+            if j >= 2:
+                v_grp[(j,)] = keep.tile([P, 2048], BF16, name="vgrpp%d" % j, align_bytes=64)
+            v_codes.append(keep.tile([P, 512], U32, name="vcod%d" % j, align_bytes=64))
+            v_scales.append(keep.tile([P, 512], U8, name="vscl%d" % j, align_bytes=64))
+            for m in range(2):
+                o_sb[(m, j)] = keep.tile([P, 2048], F32, name="osb%d%d" % (m, j))
+
+        def flip(words, dest):
+            ps = tp_pool.tile([P, 4, P], F32)
+            for w in range(4):
+                g, u = divmod(w, 2)
+                nc.tensor.transpose(ps[:, w, :], words[:, 2 * P * g + u : 2 * P * (g + 1) : 2], ident[:])
+            nc.scalar.copy(out=dest, in_=ps[:].rearrange("p (g u) r -> p g r u", g=2))
+
+        def flip_y(m, h, t):
+            if (m, h) == (0, 0):
+                dest = y_grp[(m, h, t)][:].bitcast(F32).rearrange("p (g q u) -> p g q u", g=2, u=2)
+            else:
+                dest = y_grp[(m, h)][:].bitcast(F32).rearrange("p (g t q u) -> p g t q u", g=2, t=4, u=2)[:, :, t, :, :]
+            flip(y_chunks[(m, h)][t], dest)
+
+        def flip_v(i):
+            j, c = divmod(i, 2)
+            if i < 4:
+                dest = v_grp[i][:].bitcast(F32).rearrange("p (g b u) -> p g b u", g=2, u=2)
+            else:
+                dest = v_grp[(j,)][:].bitcast(F32).rearrange("p (c g b u) -> p c g b u", c=2, g=2, u=2)[:, c, :, :, :]
+            flip(v_raw[j][:].bitcast(F32)[:, KW * c : KW * (c + 1)], dest)
+
+        def quant_y_chunk(t):
+            for g in range(2):
+                lo = 512 * g + 128 * t
+                nc.vector.quantize_mx(
+                    out=y_codes[(0, 0)][:, lo : lo + 128].bitcast(FP8X4),
+                    scales=y_scales[(0, 0)][:, lo : lo + 128],
+                    in_=y_grp[(0, 0, t)][:, 512 * g : 512 * (g + 1)],
+                )
+
+        def quant_y(m, h):
+            for g in range(2):
+                nc.vector.quantize_mx(
+                    out=y_codes[(m, h)][:, 512 * g : 512 * (g + 1)].bitcast(FP8X4),
+                    scales=y_scales[(m, h)][:, 512 * g : 512 * (g + 1)],
+                    in_=y_grp[(m, h)][:, 2048 * g : 2048 * (g + 1)],
+                )
+
+        def quant_v_chunk(i):
+            j, c = divmod(i, 2)
+            nc.vector.quantize_mx(
+                out=v_codes[j][:, 256 * c : 256 * (c + 1)].bitcast(FP8X4),
+                scales=v_scales[j][:, 256 * c : 256 * (c + 1)],
+                in_=v_grp[i][:],
+            )
+
+        def quant_v_pair(j):
+            nc.vector.quantize_mx(out=v_codes[j][:].bitcast(FP8X4), scales=v_scales[j][:], in_=v_grp[(j,)][:])
+
+        def tile_out(m, i, h):
+            j, c = divmod(i, 2)
+            acc = acc_pool.tile([P, 512], F32, tag="acc")
+            for g in range(2):
+                lo = 256 * c + 128 * g
+                nc.tensor.matmul_mx(
+                    out=acc[:],
+                    lhsT=v_codes[j][:, lo : lo + 128].bitcast(FP8X4),
+                    lhsT_scale=v_scales[j][:, lo : lo + 128],
+                    rhs=y_codes[(m, h)][:, 512 * g : 512 * (g + 1)].bitcast(FP8X4),
+                    rhs_scale=y_scales[(m, h)][:, 512 * g : 512 * (g + 1)],
+                    start=(g == 0),
+                    stop=(g == 1),
+                )
+            lo = 1024 * c + 512 * h
+            dst = o_sb[(m, j)][:, lo : lo + 512]
+            fac = v_raw[j][:, lo : lo + 512]
+            src = acc[:].rearrange("b (t q) -> b q t", t=4)
+            dst3 = dst.rearrange("b (q t) -> b q t", t=4)
+            if (m, i, h) in OFFLOAD:
+                nc.scalar.copy(out=dst3, in_=src)
+                nc.gpsimd.tensor_tensor(out=dst, in0=dst, in1=fac, op=MULT)
+            else:
+                nc.vector.tensor_tensor(out=dst3, in0=src, in1=fac.rearrange("b (q t) -> b q t", t=4), op=MULT)
+
+        def store_half_pair(m, j, h):
+            nc.sync.dma_start(
+                out=out_views[m][:, 2 * j : 2 * j + 2, 512 * h : 512 * (h + 1)],
+                in_=o_sb[(m, j)][:].rearrange("p (c r) -> p c r", c=2)[:, :, 512 * h : 512 * (h + 1)],
+            )
+
+        def store_row(m, i):
+            j, c = divmod(i, 2)
+            nc.sync.dma_start(out=out_views[m][:, i, :], in_=o_sb[(m, j)][:, 1024 * c : 1024 * (c + 1)])
+
+        def store_tile(m, i, h):
+            j, c = divmod(i, 2)
+            lo = 1024 * c + 512 * h
+            nc.sync.dma_start(out=out_views[m][:, i, 512 * h : 512 * (h + 1)], in_=o_sb[(m, j)][:, lo : lo + 512])
+
+        warm(8)
+        for t in range(4):
+            flip_y(0, 0, t)
+            quant_y_chunk(t)
+            if t % 2 == 1:
+                warm(1)
+        for i in range(3):
+            flip_v(i)
+            quant_v_chunk(i)
+            if i == 1:
+                warm(1)
+        flip_v(3)
+        warm(1)
+        tile_out(0, 0, 0)
+        quant_v_chunk(3)
+        tile_out(0, 1, 0)
+        store_half_pair(0, 0, 0)
+        flip_v(4)
+        flip_v(5)
+        tile_out(0, 2, 0)
+        quant_v_pair(2)
+        tile_out(0, 3, 0)
+        store_half_pair(0, 1, 0)
+        flip_v(6)
+        flip_v(7)
+        for t in range(4):
+            flip_y(0, 1, t)
+        quant_v_pair(3)
+        tile_out(0, 4, 0)
+        tile_out(0, 5, 0)
+        store_half_pair(0, 2, 0)
+        quant_y(0, 1)
+        tile_out(0, 6, 0)
+        tile_out(0, 7, 0)
+        store_half_pair(0, 3, 0)
+        for t in range(4):
+            flip_y(1, 0, t)
+        tile_out(0, 0, 1)
+        tile_out(0, 1, 1)
+        store_half_pair(0, 0, 1)
+        quant_y(1, 0)
+        tile_out(0, 2, 1)
+        tile_out(0, 3, 1)
+        store_half_pair(0, 1, 1)
+        for t in range(4):
+            flip_y(1, 1, t)
+        tile_out(0, 4, 1)
+        tile_out(0, 5, 1)
+        store_half_pair(0, 2, 1)
+        quant_y(1, 1)
+        tile_out(0, 6, 1)
+        tile_out(0, 7, 1)
+        store_half_pair(0, 3, 1)
+        for i in range(7):
+            tile_out(1, i, 0)
+            tile_out(1, i, 1)
+            store_row(1, i)
+        for h in range(2):
+            tile_out(1, 7, h)
+            store_tile(1, 7, h)

@@ -15,6 +15,7 @@ K = 1024
 KW = K // 2
 FLOPS = 2 * 2 * 1024 * 1024 * 1024
 
+SORTED = ((0, 1), (1, 0), (1, 1))
 OFFLOAD = ((1, 0, 0), (1, 2, 0), (1, 4, 0), (1, 6, 0))
 
 
@@ -51,12 +52,14 @@ def tile_pinnlayer_pb_kernel(tc, Volt, Y, Yconj, out_0, out_1):
             chunks = []
             for s in range(pieces):
                 raw = load(view[:, per * s : per * (s + 1), :], per, "yraw%d%d%d" % (m, h, s))
+                y_raw[(m, h)] = raw
                 words = raw[:].bitcast(F32)
                 for t in range(per):
                     chunks.append(words[:, KW * t : KW * (t + 1)])
             return chunks
 
         y_chunks = {}
+        y_raw = {}
         v_raw = []
         y_chunks[(0, 0)] = load_half(0, 0, 2)
         for j in range(4):
@@ -91,11 +94,29 @@ def tile_pinnlayer_pb_kernel(tc, Volt, Y, Yconj, out_0, out_1):
             for m in range(2):
                 o_sb[(m, j)] = keep.tile([P, 2048], F32, name="osb%d%d" % (m, j))
 
-        def flip(words, dest):
+        sorted_words = {}
+        for m, h in SORTED:
+            sorted_words[(m, h)] = keep.tile([P, 2048], F32, name="ysrt%d%d" % (m, h))
+
+        def sort_y(m, h):
+            for s in range(2):
+                lo = 1024 * s
+                src = y_raw[(m, h)][:].bitcast(F32)[:, lo : lo + 1024]
+                dst = sorted_words[(m, h)][:, lo : lo + 1024]
+                nc.scalar.copy(
+                    out=dst.rearrange("p (x u q) -> p x u q", u=2, q=P),
+                    in_=src.rearrange("p (x q u) -> p x u q", u=2, q=P),
+                )
+
+        def flip(words, dest, in_order):
             ps = tp_pool.tile([P, 4, P], F32)
             for w in range(4):
                 g, u = divmod(w, 2)
-                nc.tensor.transpose(ps[:, w, :], words[:, 2 * P * g + u : 2 * P * (g + 1) : 2], ident[:])
+                if in_order:
+                    piece = words[:, P * w : P * (w + 1)]
+                else:
+                    piece = words[:, 2 * P * g + u : 2 * P * (g + 1) : 2]
+                nc.tensor.transpose(ps[:, w, :], piece, ident[:])
             nc.scalar.copy(out=dest, in_=ps[:].rearrange("p (g u) r -> p g r u", g=2))
 
         def flip_y(m, h, t):
@@ -103,7 +124,10 @@ def tile_pinnlayer_pb_kernel(tc, Volt, Y, Yconj, out_0, out_1):
                 dest = y_grp[(m, h, t)][:].bitcast(F32).rearrange("p (g q u) -> p g q u", g=2, u=2)
             else:
                 dest = y_grp[(m, h)][:].bitcast(F32).rearrange("p (g t q u) -> p g t q u", g=2, t=4, u=2)[:, :, t, :, :]
-            flip(y_chunks[(m, h)][t], dest)
+            if (m, h) in SORTED:
+                flip(sorted_words[(m, h)][:, KW * t : KW * (t + 1)], dest, True)
+            else:
+                flip(y_chunks[(m, h)][t], dest, False)
 
         def flip_v(i):
             j, c = divmod(i, 2)
@@ -111,7 +135,7 @@ def tile_pinnlayer_pb_kernel(tc, Volt, Y, Yconj, out_0, out_1):
                 dest = v_grp[i][:].bitcast(F32).rearrange("p (g b u) -> p g b u", g=2, u=2)
             else:
                 dest = v_grp[(j,)][:].bitcast(F32).rearrange("p (c g b u) -> p c g b u", c=2, g=2, u=2)[:, c, :, :, :]
-            flip(v_raw[j][:].bitcast(F32)[:, KW * c : KW * (c + 1)], dest)
+            flip(v_raw[j][:].bitcast(F32)[:, KW * c : KW * (c + 1)], dest, False)
 
         def quant_y_chunk(t):
             for g in range(2):
@@ -200,6 +224,7 @@ def tile_pinnlayer_pb_kernel(tc, Volt, Y, Yconj, out_0, out_1):
         store_half_pair(0, 0, 0)
         flip_v(4)
         flip_v(5)
+        sort_y(0, 1)
         tile_out(0, 2, 0)
         quant_v_pair(2)
         tile_out(0, 3, 0)
@@ -208,6 +233,7 @@ def tile_pinnlayer_pb_kernel(tc, Volt, Y, Yconj, out_0, out_1):
         flip_v(7)
         for t in range(4):
             flip_y(0, 1, t)
+        sort_y(1, 0)
         quant_v_pair(3)
         tile_out(0, 4, 0)
         tile_out(0, 5, 0)
@@ -218,6 +244,7 @@ def tile_pinnlayer_pb_kernel(tc, Volt, Y, Yconj, out_0, out_1):
         store_half_pair(0, 3, 0)
         for t in range(4):
             flip_y(1, 0, t)
+        sort_y(1, 1)
         tile_out(0, 0, 1)
         tile_out(0, 1, 1)
         store_half_pair(0, 0, 1)

@@ -15,8 +15,9 @@ K = 1024
 KW = K // 2
 FLOPS = 2 * 2 * 1024 * 1024 * 1024
 
-SORTED = ((0, 1), (1, 0), (1, 1))
 OFFLOAD = ((1, 0, 0), (1, 2, 0), (1, 4, 0), (1, 6, 0))
+SORTED_V = (2, 3)
+SORTED_Y = ((0, 1), (1, 0), (1, 1))
 
 
 def tile_pinnlayer_pb_kernel(tc, Volt, Y, Yconj, out_0, out_1):
@@ -49,28 +50,23 @@ def tile_pinnlayer_pb_kernel(tc, Volt, Y, Yconj, out_0, out_1):
         def load_half(m, h, pieces):
             view = mats[m][512 * h : 512 * (h + 1), :].rearrange("(q t) k -> q t k", t=4)
             per = 4 // pieces
-            chunks = []
-            for s in range(pieces):
-                raw = load(view[:, per * s : per * (s + 1), :], per, "yraw%d%d%d" % (m, h, s))
-                y_raw[(m, h)] = raw
-                words = raw[:].bitcast(F32)
-                for t in range(per):
-                    chunks.append(words[:, KW * t : KW * (t + 1)])
-            return chunks
+            return [load(view[:, per * s : per * (s + 1), :], per, "yraw%d%d%d" % (m, h, s)) for s in range(pieces)]
 
-        y_chunks = {}
+        def words_of(pieces, t):
+            per = 4 // len(pieces)
+            s, r = divmod(t, per)
+            return pieces[s][:].bitcast(F32)[:, KW * r : KW * (r + 1)]
+
         y_raw = {}
-        v_raw = []
-        y_chunks[(0, 0)] = load_half(0, 0, 2)
-        for j in range(4):
-            v_raw.append(load(volt_view[:, 2 * j : 2 * j + 2, :], 2, "vraw%d" % j))
-        y_chunks[(0, 1)] = load_half(0, 1, 1)
-        y_chunks[(1, 0)] = load_half(1, 0, 1)
-        y_chunks[(1, 1)] = load_half(1, 1, 1)
+        y_raw[(0, 0)] = load_half(0, 0, 4)
+        v_raw = [load(volt_view[:, 2 * j : 2 * j + 2, :], 2, "vraw%d" % j) for j in range(4)]
+        for m, h in ((0, 1), (1, 0), (1, 1)):
+            y_raw[(m, h)] = load_half(m, h, 2)
 
         y_grp = {}
         y_codes = {}
         y_scales = {}
+        y_srt = {}
         for m in range(2):
             for h in range(2):
                 if (m, h) == (0, 0):
@@ -78,9 +74,12 @@ def tile_pinnlayer_pb_kernel(tc, Volt, Y, Yconj, out_0, out_1):
                         y_grp[(m, h, t)] = keep.tile([P, 1024], BF16, name="ygrp%d%d%d" % (m, h, t), align_bytes=64)
                 else:
                     y_grp[(m, h)] = keep.tile([P, 4096], BF16, name="ygrp%d%d" % (m, h), align_bytes=64)
+                if (m, h) in SORTED_Y:
+                    y_srt[(m, h)] = [keep.tile([P, 1024], F32, name="ysrt%d%d%d" % (m, h, s)) for s in range(2)]
                 y_codes[(m, h)] = keep.tile([P, 1024], U32, name="ycod%d%d" % (m, h), align_bytes=64)
                 y_scales[(m, h)] = keep.tile([P, 1024], U8, name="yscl%d%d" % (m, h), align_bytes=64)
         v_grp = {}
+        v_srt = {}
         v_codes = []
         v_scales = []
         o_sb = {}
@@ -89,24 +88,27 @@ def tile_pinnlayer_pb_kernel(tc, Volt, Y, Yconj, out_0, out_1):
         for j in range(4):
             if j >= 2:
                 v_grp[(j,)] = keep.tile([P, 2048], BF16, name="vgrpp%d" % j, align_bytes=64)
+            if j in SORTED_V:
+                v_srt[j] = keep.tile([P, 1024], F32, name="vsrt%d" % j)
             v_codes.append(keep.tile([P, 512], U32, name="vcod%d" % j, align_bytes=64))
             v_scales.append(keep.tile([P, 512], U8, name="vscl%d" % j, align_bytes=64))
             for m in range(2):
                 o_sb[(m, j)] = keep.tile([P, 2048], F32, name="osb%d%d" % (m, j))
 
-        sorted_words = {}
-        for m, h in SORTED:
-            sorted_words[(m, h)] = keep.tile([P, 2048], F32, name="ysrt%d%d" % (m, h))
+        def sort_words(copy, raw, srt):
+            copy(
+                out=srt[:].rearrange("p (x u q) -> p x u q", u=2, q=P),
+                in_=raw[:].bitcast(F32).rearrange("p (x q u) -> p x u q", u=2, q=P),
+            )
 
-        def sort_y(m, h):
-            for s in range(2):
-                lo = 1024 * s
-                src = y_raw[(m, h)][:].bitcast(F32)[:, lo : lo + 1024]
-                dst = sorted_words[(m, h)][:, lo : lo + 1024]
-                nc.scalar.copy(
-                    out=dst.rearrange("p (x u q) -> p x u q", u=2, q=P),
-                    in_=src.rearrange("p (x q u) -> p x u q", u=2, q=P),
-                )
+        def sort_y(copy, m, h, s):
+            sort_words(copy, y_raw[(m, h)][s], y_srt[(m, h)][s])
+
+        def sort_v(copy, j):
+            sort_words(copy, v_raw[j], v_srt[j])
+
+        on_v = nc.vector.tensor_copy
+        on_s = nc.scalar.copy
 
         def flip(words, dest, in_order):
             ps = tp_pool.tile([P, 4, P], F32)
@@ -124,10 +126,11 @@ def tile_pinnlayer_pb_kernel(tc, Volt, Y, Yconj, out_0, out_1):
                 dest = y_grp[(m, h, t)][:].bitcast(F32).rearrange("p (g q u) -> p g q u", g=2, u=2)
             else:
                 dest = y_grp[(m, h)][:].bitcast(F32).rearrange("p (g t q u) -> p g t q u", g=2, t=4, u=2)[:, :, t, :, :]
-            if (m, h) in SORTED:
-                flip(sorted_words[(m, h)][:, KW * t : KW * (t + 1)], dest, True)
+            if (m, h) in SORTED_Y:
+                s, c = divmod(t, 2)
+                flip(y_srt[(m, h)][s][:, KW * c : KW * (c + 1)], dest, True)
             else:
-                flip(y_chunks[(m, h)][t], dest, False)
+                flip(words_of(y_raw[(m, h)], t), dest, False)
 
         def flip_v(i):
             j, c = divmod(i, 2)
@@ -135,7 +138,10 @@ def tile_pinnlayer_pb_kernel(tc, Volt, Y, Yconj, out_0, out_1):
                 dest = v_grp[i][:].bitcast(F32).rearrange("p (g b u) -> p g b u", g=2, u=2)
             else:
                 dest = v_grp[(j,)][:].bitcast(F32).rearrange("p (c g b u) -> p c g b u", c=2, g=2, u=2)[:, c, :, :, :]
-            flip(v_raw[j][:].bitcast(F32)[:, KW * c : KW * (c + 1)], dest, False)
+            if j in SORTED_V:
+                flip(v_srt[j][:, KW * c : KW * (c + 1)], dest, True)
+            else:
+                flip(v_raw[j][:].bitcast(F32)[:, KW * c : KW * (c + 1)], dest, False)
 
         def quant_y_chunk(t):
             for g in range(2):
@@ -190,81 +196,79 @@ def tile_pinnlayer_pb_kernel(tc, Volt, Y, Yconj, out_0, out_1):
             else:
                 nc.vector.tensor_tensor(out=dst3, in0=src, in1=fac.rearrange("b (q t) -> b q t", t=4), op=MULT)
 
-        def store_half_pair(m, j, h):
+        def store_pair(m, j, h):
             nc.sync.dma_start(
                 out=out_views[m][:, 2 * j : 2 * j + 2, 512 * h : 512 * (h + 1)],
                 in_=o_sb[(m, j)][:].rearrange("p (c r) -> p c r", c=2)[:, :, 512 * h : 512 * (h + 1)],
             )
-
-        def store_row(m, i):
-            j, c = divmod(i, 2)
-            nc.sync.dma_start(out=out_views[m][:, i, :], in_=o_sb[(m, j)][:, 1024 * c : 1024 * (c + 1)])
 
         def store_tile(m, i, h):
             j, c = divmod(i, 2)
             lo = 1024 * c + 512 * h
             nc.sync.dma_start(out=out_views[m][:, i, 512 * h : 512 * (h + 1)], in_=o_sb[(m, j)][:, lo : lo + 512])
 
+        def two(m, j, h):
+            tile_out(m, 2 * j, h)
+            tile_out(m, 2 * j + 1, h)
+            store_pair(m, j, h)
+
         warm(8)
         for t in range(4):
             flip_y(0, 0, t)
             quant_y_chunk(t)
-            if t % 2 == 1:
-                warm(1)
-        for i in range(3):
+        for i in range(4):
+            if i == 2:
+                sort_v(on_v, 2)
             flip_v(i)
             quant_v_chunk(i)
-            if i == 1:
-                warm(1)
-        flip_v(3)
-        warm(1)
         tile_out(0, 0, 0)
-        quant_v_chunk(3)
+        sort_v(on_v, 3)
         tile_out(0, 1, 0)
-        store_half_pair(0, 0, 0)
+        store_pair(0, 0, 0)
         flip_v(4)
         flip_v(5)
-        sort_y(0, 1)
-        tile_out(0, 2, 0)
         quant_v_pair(2)
+        sort_y(on_v, 0, 1, 0)
+        tile_out(0, 2, 0)
+        sort_y(on_v, 0, 1, 1)
         tile_out(0, 3, 0)
-        store_half_pair(0, 1, 0)
+        store_pair(0, 1, 0)
         flip_v(6)
         flip_v(7)
-        for t in range(4):
-            flip_y(0, 1, t)
-        sort_y(1, 0)
         quant_v_pair(3)
+        flip_y(0, 1, 0)
+        flip_y(0, 1, 1)
         tile_out(0, 4, 0)
+        sort_y(on_v, 1, 0, 0)
         tile_out(0, 5, 0)
-        store_half_pair(0, 2, 0)
+        store_pair(0, 2, 0)
+        flip_y(0, 1, 2)
+        flip_y(0, 1, 3)
         quant_y(0, 1)
         tile_out(0, 6, 0)
+        sort_y(on_v, 1, 0, 1)
         tile_out(0, 7, 0)
-        store_half_pair(0, 3, 0)
-        for t in range(4):
-            flip_y(1, 0, t)
-        sort_y(1, 1)
-        tile_out(0, 0, 1)
-        tile_out(0, 1, 1)
-        store_half_pair(0, 0, 1)
+        store_pair(0, 3, 0)
+        flip_y(1, 0, 0)
+        flip_y(1, 0, 1)
+        sort_y(on_s, 1, 1, 0)
+        two(0, 0, 1)
+        flip_y(1, 0, 2)
+        flip_y(1, 0, 3)
         quant_y(1, 0)
-        tile_out(0, 2, 1)
-        tile_out(0, 3, 1)
-        store_half_pair(0, 1, 1)
-        for t in range(4):
-            flip_y(1, 1, t)
-        tile_out(0, 4, 1)
-        tile_out(0, 5, 1)
-        store_half_pair(0, 2, 1)
+        sort_y(on_s, 1, 1, 1)
+        two(0, 1, 1)
+        flip_y(1, 1, 0)
+        flip_y(1, 1, 1)
+        two(0, 2, 1)
+        flip_y(1, 1, 2)
+        flip_y(1, 1, 3)
         quant_y(1, 1)
-        tile_out(0, 6, 1)
-        tile_out(0, 7, 1)
-        store_half_pair(0, 3, 1)
-        for i in range(7):
-            tile_out(1, i, 0)
+        two(0, 3, 1)
+        for j in range(4):
+            two(1, j, 0)
+        for j in range(3):
+            two(1, j, 1)
+        for i in range(6, 8):
             tile_out(1, i, 1)
-            store_row(1, i)
-        for h in range(2):
-            tile_out(1, 7, h)
-            store_tile(1, 7, h)
+            store_tile(1, i, 1)

@@ -15,9 +15,24 @@ K = 1024
 KW = K // 2
 FLOPS = 2 * 2 * 1024 * 1024 * 1024
 
-OFFLOAD = ((1, 0, 0), (1, 2, 0), (1, 4, 0), (1, 6, 0))
-SORTED_V = (2, 3)
-SORTED_Y = ((0, 1), (1, 0), (1, 1))
+OFFLOAD = ((1, 1, 0), (1, 3, 0), (1, 5, 0), (1, 6, 0))
+SORTED_V = (2, 3, 4, 5, 6, 7)
+SORTED_Y = ((1, 0), (1, 1))
+LOADS = (
+    ("y", 0, 0, (0,)),
+    ("y", 0, 0, (1,)),
+    ("y", 0, 0, (2, 3)),
+    ("v", (0, 1)),
+    ("y", 0, 1, (0, 1)),
+    ("y", 0, 1, (2, 3)),
+    ("v", (2, 3)),
+    ("v", (4, 5)),
+    ("v", (6, 7)),
+    ("y", 1, 0, (0, 1)),
+    ("y", 1, 0, (2, 3)),
+    ("y", 1, 1, (0, 1)),
+    ("y", 1, 1, (2, 3)),
+)
 
 
 def tile_pinnlayer_pb_kernel(tc, Volt, Y, Yconj, out_0, out_1):
@@ -42,153 +57,126 @@ def tile_pinnlayer_pb_kernel(tc, Volt, Y, Yconj, out_0, out_1):
                 w = acc_pool.tile([P, 512], F32, tag="acc", name="warm")
                 nc.tensor.matmul(out=w[:], lhsT=zeros[:, 0:P], rhs=zeros[:], start=True, stop=True)
 
-        def load(view, rows, name):
-            raw = keep.tile([P, rows * K], BF16, name=name)
-            nc.sync.dma_start(out=raw[:].rearrange("p (t k) -> p t k", t=rows), in_=view)
-            return raw
+        home = {}
+        pieces = {}
+        for load in LOADS:
+            first = load[-1][0]
+            rows = len(load[-1])
+            if load[0] == "y":
+                m, h = load[1:3]
+                view = mats[m][512 * h : 512 * (h + 1), :].rearrange("(q t) k -> q t k", t=4)
+                chunks = [("y", m, h, t) for t in load[-1]]
+                name = "y%d%d%d" % (m, h, first)
+            else:
+                view = volt_view
+                chunks = [("v", i) for i in load[-1]]
+                name = "v%d" % first
+            raw = keep.tile([P, rows * K], BF16, name="raw" + name)
+            nc.sync.dma_start(out=raw[:].rearrange("p (t k) -> p t k", t=rows), in_=view[:, first : first + rows, :])
+            for n in range(rows):
+                home[chunks[n]] = (raw, n)
 
-        def load_half(m, h, pieces):
-            view = mats[m][512 * h : 512 * (h + 1), :].rearrange("(q t) k -> q t k", t=4)
-            per = 4 // pieces
-            return [load(view[:, per * s : per * (s + 1), :], per, "yraw%d%d%d" % (m, h, s)) for s in range(pieces)]
+        def words(chunk):
+            raw, n = home[chunk]
+            return raw[:].bitcast(F32)[:, KW * n : KW * (n + 1)]
 
-        def words_of(pieces, t):
-            per = 4 // len(pieces)
-            s, r = divmod(t, per)
-            return pieces[s][:].bitcast(F32)[:, KW * r : KW * (r + 1)]
+        def volt_row(i):
+            raw, n = home[("v", i)]
+            return raw[:, K * n : K * (n + 1)]
 
-        y_raw = {}
-        y_raw[(0, 0)] = load_half(0, 0, 4)
-        v_raw = [load(volt_view[:, 2 * j : 2 * j + 2, :], 2, "vraw%d" % j) for j in range(4)]
-        for m, h in ((0, 1), (1, 0), (1, 1)):
-            y_raw[(m, h)] = load_half(m, h, 2)
-
-        y_grp = {}
-        y_codes = {}
-        y_scales = {}
-        y_srt = {}
+        grp = {}
+        codes = {}
+        scales = {}
+        o_sb = {}
         for m in range(2):
             for h in range(2):
-                if (m, h) == (0, 0):
-                    for t in range(4):
-                        y_grp[(m, h, t)] = keep.tile([P, 1024], BF16, name="ygrp%d%d%d" % (m, h, t), align_bytes=64)
-                else:
-                    y_grp[(m, h)] = keep.tile([P, 4096], BF16, name="ygrp%d%d" % (m, h), align_bytes=64)
-                if (m, h) in SORTED_Y:
-                    y_srt[(m, h)] = [keep.tile([P, 1024], F32, name="ysrt%d%d%d" % (m, h, s)) for s in range(2)]
-                y_codes[(m, h)] = keep.tile([P, 1024], U32, name="ycod%d%d" % (m, h), align_bytes=64)
-                y_scales[(m, h)] = keep.tile([P, 1024], U8, name="yscl%d%d" % (m, h), align_bytes=64)
-        v_grp = {}
-        v_srt = {}
-        v_codes = []
-        v_scales = []
-        o_sb = {}
-        for i in range(4):
-            v_grp[i] = keep.tile([P, 1024], BF16, name="vgrpc%d" % i, align_bytes=64)
-        for j in range(4):
-            if j >= 2:
-                v_grp[(j,)] = keep.tile([P, 2048], BF16, name="vgrpp%d" % j, align_bytes=64)
-            if j in SORTED_V:
-                v_srt[j] = keep.tile([P, 1024], F32, name="vsrt%d" % j)
-            v_codes.append(keep.tile([P, 512], U32, name="vcod%d" % j, align_bytes=64))
-            v_scales.append(keep.tile([P, 512], U8, name="vscl%d" % j, align_bytes=64))
-            for m in range(2):
+                grp[(m, h)] = keep.tile([P, 4096], BF16, name="ygrp%d%d" % (m, h), align_bytes=64)
+                codes[(m, h)] = keep.tile([P, 1024], U32, name="ycod%d%d" % (m, h), align_bytes=64)
+                scales[(m, h)] = keep.tile([P, 1024], U8, name="yscl%d%d" % (m, h), align_bytes=64)
+            for j in range(4):
                 o_sb[(m, j)] = keep.tile([P, 2048], F32, name="osb%d%d" % (m, j))
+        for j in range(4):
+            grp[j] = keep.tile([P, 2048], BF16, name="vgrp%d" % j, align_bytes=64)
+            codes[j] = keep.tile([P, 512], U32, name="vcod%d" % j, align_bytes=64)
+            scales[j] = keep.tile([P, 512], U8, name="vscl%d" % j, align_bytes=64)
 
-        def sort_words(copy, raw, srt):
+        ON_V = nc.vector.tensor_copy
+        ON_S = nc.scalar.copy
+        ordered = {}
+
+        def sort(copy, chunks):
+            raw, n = home[chunks[0]]
+            srt = keep.tile([P, KW * len(chunks)], F32, name="srt" + "".join(str(x) for x in chunks[0]))
             copy(
                 out=srt[:].rearrange("p (x u q) -> p x u q", u=2, q=P),
-                in_=raw[:].bitcast(F32).rearrange("p (x q u) -> p x u q", u=2, q=P),
+                in_=raw[:].bitcast(F32)[:, KW * n : KW * (n + len(chunks))].rearrange("p (x q u) -> p x u q", u=2, q=P),
             )
+            for c in range(len(chunks)):
+                ordered[chunks[c]] = srt[:, KW * c : KW * (c + 1)]
 
-        def sort_y(copy, m, h, s):
-            sort_words(copy, y_raw[(m, h)][s], y_srt[(m, h)][s])
+        def sort_y(copy, m, h, *ts):
+            sort(copy, [("y", m, h, t) for t in ts])
 
-        def sort_v(copy, j):
-            sort_words(copy, v_raw[j], v_srt[j])
+        def sort_v(copy, *rows):
+            sort(copy, [("v", i) for i in rows])
 
-        on_v = nc.vector.tensor_copy
-        on_s = nc.scalar.copy
-
-        def flip(words, dest, in_order):
+        def flip(chunk, dest, in_order):
             ps = tp_pool.tile([P, 4, P], F32)
             for w in range(4):
                 g, u = divmod(w, 2)
                 if in_order:
-                    piece = words[:, P * w : P * (w + 1)]
+                    piece = ordered[chunk][:, P * w : P * (w + 1)]
                 else:
-                    piece = words[:, 2 * P * g + u : 2 * P * (g + 1) : 2]
+                    piece = words(chunk)[:, 2 * P * g + u : 2 * P * (g + 1) : 2]
                 nc.tensor.transpose(ps[:, w, :], piece, ident[:])
             nc.scalar.copy(out=dest, in_=ps[:].rearrange("p (g u) r -> p g r u", g=2))
 
         def flip_y(m, h, t):
-            if (m, h) == (0, 0):
-                dest = y_grp[(m, h, t)][:].bitcast(F32).rearrange("p (g q u) -> p g q u", g=2, u=2)
-            else:
-                dest = y_grp[(m, h)][:].bitcast(F32).rearrange("p (g t q u) -> p g t q u", g=2, t=4, u=2)[:, :, t, :, :]
-            if (m, h) in SORTED_Y:
-                s, c = divmod(t, 2)
-                flip(y_srt[(m, h)][s][:, KW * c : KW * (c + 1)], dest, True)
-            else:
-                flip(words_of(y_raw[(m, h)], t), dest, False)
+            dest = grp[(m, h)][:].bitcast(F32).rearrange("p (g t q u) -> p g t q u", g=2, t=4, u=2)[:, :, t, :, :]
+            flip(("y", m, h, t), dest, (m, h) in SORTED_Y)
 
         def flip_v(i):
             j, c = divmod(i, 2)
-            if i < 4:
-                dest = v_grp[i][:].bitcast(F32).rearrange("p (g b u) -> p g b u", g=2, u=2)
-            else:
-                dest = v_grp[(j,)][:].bitcast(F32).rearrange("p (c g b u) -> p c g b u", c=2, g=2, u=2)[:, c, :, :, :]
-            if j in SORTED_V:
-                flip(v_srt[j][:, KW * c : KW * (c + 1)], dest, True)
-            else:
-                flip(v_raw[j][:].bitcast(F32)[:, KW * c : KW * (c + 1)], dest, False)
+            dest = grp[j][:].bitcast(F32).rearrange("p (c g b u) -> p c g b u", c=2, g=2, u=2)[:, c, :, :, :]
+            flip(("v", i), dest, i in SORTED_V)
 
-        def quant_y_chunk(t):
+        def quant_y(m, h, *ts):
             for g in range(2):
-                lo = 512 * g + 128 * t
+                lo = 512 * g + P * ts[0]
+                hi = lo + P * len(ts)
                 nc.vector.quantize_mx(
-                    out=y_codes[(0, 0)][:, lo : lo + 128].bitcast(FP8X4),
-                    scales=y_scales[(0, 0)][:, lo : lo + 128],
-                    in_=y_grp[(0, 0, t)][:, 512 * g : 512 * (g + 1)],
+                    out=codes[(m, h)][:, lo:hi].bitcast(FP8X4), scales=scales[(m, h)][:, lo:hi], in_=grp[(m, h)][:, 4 * lo : 4 * hi]
                 )
 
-        def quant_y(m, h):
-            for g in range(2):
-                nc.vector.quantize_mx(
-                    out=y_codes[(m, h)][:, 512 * g : 512 * (g + 1)].bitcast(FP8X4),
-                    scales=y_scales[(m, h)][:, 512 * g : 512 * (g + 1)],
-                    in_=y_grp[(m, h)][:, 2048 * g : 2048 * (g + 1)],
-                )
+        def quant_v(*rows):
+            j, c = divmod(rows[0], 2)
+            lo = 256 * c
+            hi = lo + 256 * len(rows)
+            nc.vector.quantize_mx(out=codes[j][:, lo:hi].bitcast(FP8X4), scales=scales[j][:, lo:hi], in_=grp[j][:, 4 * lo : 4 * hi])
 
-        def quant_v_chunk(i):
+        sums = {}
+
+        def mx(m, i, h):
             j, c = divmod(i, 2)
-            nc.vector.quantize_mx(
-                out=v_codes[j][:, 256 * c : 256 * (c + 1)].bitcast(FP8X4),
-                scales=v_scales[j][:, 256 * c : 256 * (c + 1)],
-                in_=v_grp[i][:],
-            )
-
-        def quant_v_pair(j):
-            nc.vector.quantize_mx(out=v_codes[j][:].bitcast(FP8X4), scales=v_scales[j][:], in_=v_grp[(j,)][:])
-
-        def tile_out(m, i, h):
-            j, c = divmod(i, 2)
-            acc = acc_pool.tile([P, 512], F32, tag="acc")
+            acc = acc_pool.tile([P, 512], F32, tag="acc", name="acc")
             for g in range(2):
-                lo = 256 * c + 128 * g
+                lo = 256 * c + P * g
                 nc.tensor.matmul_mx(
                     out=acc[:],
-                    lhsT=v_codes[j][:, lo : lo + 128].bitcast(FP8X4),
-                    lhsT_scale=v_scales[j][:, lo : lo + 128],
-                    rhs=y_codes[(m, h)][:, 512 * g : 512 * (g + 1)].bitcast(FP8X4),
-                    rhs_scale=y_scales[(m, h)][:, 512 * g : 512 * (g + 1)],
+                    lhsT=codes[j][:, lo : lo + P].bitcast(FP8X4),
+                    lhsT_scale=scales[j][:, lo : lo + P],
+                    rhs=codes[(m, h)][:, 512 * g : 512 * (g + 1)].bitcast(FP8X4),
+                    rhs_scale=scales[(m, h)][:, 512 * g : 512 * (g + 1)],
                     start=(g == 0),
                     stop=(g == 1),
                 )
-            lo = 1024 * c + 512 * h
-            dst = o_sb[(m, j)][:, lo : lo + 512]
-            fac = v_raw[j][:, lo : lo + 512]
-            src = acc[:].rearrange("b (t q) -> b q t", t=4)
+            sums[(m, i, h)] = acc
+
+        def product(m, i, h):
+            j, c = divmod(i, 2)
+            dst = o_sb[(m, j)][:, 1024 * c + 512 * h : 1024 * c + 512 * (h + 1)]
+            fac = volt_row(i)[:, 512 * h : 512 * (h + 1)]
+            src = sums[(m, i, h)][:].rearrange("b (t q) -> b q t", t=4)
             dst3 = dst.rearrange("b (q t) -> b q t", t=4)
             if (m, i, h) in OFFLOAD:
                 nc.scalar.copy(out=dst3, in_=src)
@@ -196,10 +184,12 @@ def tile_pinnlayer_pb_kernel(tc, Volt, Y, Yconj, out_0, out_1):
             else:
                 nc.vector.tensor_tensor(out=dst3, in0=src, in1=fac.rearrange("b (q t) -> b q t", t=4), op=MULT)
 
-        def store_pair(m, j, h):
+        def store_rows(m, *rows):
+            j, c = divmod(rows[0], 2)
+            lo = 1024 * c
+            hi = lo + 1024 * len(rows)
             nc.sync.dma_start(
-                out=out_views[m][:, 2 * j : 2 * j + 2, 512 * h : 512 * (h + 1)],
-                in_=o_sb[(m, j)][:].rearrange("p (c r) -> p c r", c=2)[:, :, 512 * h : 512 * (h + 1)],
+                out=out_views[m][:, rows[0] : rows[0] + len(rows), :], in_=o_sb[(m, j)][:, lo:hi].rearrange("p (c r) -> p c r", r=1024)
             )
 
         def store_tile(m, i, h):
@@ -207,68 +197,72 @@ def tile_pinnlayer_pb_kernel(tc, Volt, Y, Yconj, out_0, out_1):
             lo = 1024 * c + 512 * h
             nc.sync.dma_start(out=out_views[m][:, i, 512 * h : 512 * (h + 1)], in_=o_sb[(m, j)][:, lo : lo + 512])
 
-        def two(m, j, h):
-            tile_out(m, 2 * j, h)
-            tile_out(m, 2 * j + 1, h)
-            store_pair(m, j, h)
-
+        def row(m, i, split=False):
+            for h in range(2):
+                mx(m, i, h)
+            for h in range(2):
+                product(m, i, h)
+                if split:
+                    store_tile(m, i, h)
+            if not split:
+                store_rows(m, i)
         warm(8)
         for t in range(4):
             flip_y(0, 0, t)
-            quant_y_chunk(t)
-        for i in range(4):
-            if i == 2:
-                sort_v(on_v, 2)
+            quant_y(0, 0, t)
+        for i in range(2):
             flip_v(i)
-            quant_v_chunk(i)
-        tile_out(0, 0, 0)
-        sort_v(on_v, 3)
-        tile_out(0, 1, 0)
-        store_pair(0, 0, 0)
-        flip_v(4)
-        flip_v(5)
-        quant_v_pair(2)
-        sort_y(on_v, 0, 1, 0)
-        tile_out(0, 2, 0)
-        sort_y(on_v, 0, 1, 1)
-        tile_out(0, 3, 0)
-        store_pair(0, 1, 0)
+            quant_v(i)
+        for t in range(4):
+            flip_y(0, 1, t)
+            if t == 2:
+                sort_v(ON_V, 2, 3)
+            quant_y(0, 1, t)
+        mx(0, 0, 0)
+        mx(0, 1, 0)
+        sort_v(ON_V, 4, 5)
+        product(0, 0, 0)
+        product(0, 1, 0)
+        for i in range(2, 6):
+            flip_v(i)
+        quant_v(2, 3)
+        sort_v(ON_V, 6, 7)
+        quant_v(4, 5)
+        sort_y(ON_S, 1, 0, 0, 1)
+        mx(0, 0, 1)
+        mx(0, 1, 1)
+        product(0, 0, 1)
+        store_rows(0, 0)
+        product(0, 1, 1)
+        store_rows(0, 1)
+        row(0, 2)
         flip_v(6)
         flip_v(7)
-        quant_v_pair(3)
-        flip_y(0, 1, 0)
-        flip_y(0, 1, 1)
-        tile_out(0, 4, 0)
-        sort_y(on_v, 1, 0, 0)
-        tile_out(0, 5, 0)
-        store_pair(0, 2, 0)
-        flip_y(0, 1, 2)
-        flip_y(0, 1, 3)
-        quant_y(0, 1)
-        tile_out(0, 6, 0)
-        sort_y(on_v, 1, 0, 1)
-        tile_out(0, 7, 0)
-        store_pair(0, 3, 0)
-        flip_y(1, 0, 0)
-        flip_y(1, 0, 1)
-        sort_y(on_s, 1, 1, 0)
-        two(0, 0, 1)
-        flip_y(1, 0, 2)
-        flip_y(1, 0, 3)
-        quant_y(1, 0)
-        sort_y(on_s, 1, 1, 1)
-        two(0, 1, 1)
-        flip_y(1, 1, 0)
-        flip_y(1, 1, 1)
-        two(0, 2, 1)
-        flip_y(1, 1, 2)
-        flip_y(1, 1, 3)
-        quant_y(1, 1)
-        two(0, 3, 1)
-        for j in range(4):
-            two(1, j, 0)
-        for j in range(3):
-            two(1, j, 1)
-        for i in range(6, 8):
-            tile_out(1, i, 1)
-            store_tile(1, i, 1)
+        quant_v(6, 7)
+        sort_y(ON_S, 1, 0, 2, 3)
+        row(0, 3)
+        row(0, 4)
+        sort_y(ON_S, 1, 1, 0, 1)
+        for t in range(4):
+            flip_y(1, 0, t)
+        quant_y(1, 0, 0, 1)
+        sort_y(ON_S, 1, 1, 2, 3)
+        row(0, 5)
+        quant_y(1, 0, 2, 3)
+        row(0, 6)
+        for t in range(4):
+            flip_y(1, 1, t)
+        row(0, 7)
+        quant_y(1, 1, 0, 1)
+        mx(1, 0, 0)
+        mx(1, 1, 0)
+        quant_y(1, 1, 2, 3)
+        product(1, 0, 0)
+        product(1, 1, 0)
+        for i in range(2):
+            mx(1, i, 1)
+            product(1, i, 1)
+            store_rows(1, i)
+        for i in range(2, 7):
+            row(1, i)
+        row(1, 7, True)

@@ -18,6 +18,8 @@ FLOPS = 2 * 2 * 1024 * 1024 * 1024
 OFFLOAD = ((1, 1, 0), (1, 3, 0), (1, 5, 0), (1, 6, 0))
 SORTED_V = (2, 3, 4, 5, 6, 7)
 SORTED_Y = ((1, 0), (1, 1))
+Y_GROUPS = ((0, 0, (0,)), (0, 0, (1,)), (0, 0, (2,)), (0, 0, (3,)), (0, 1, (0,)), (0, 1, (1,)), (0, 1, (2,)), (0, 1, (3,)), (1, 0, (0, 1)), (1, 0, (2, 3)), (1, 1, (0, 1)), (1, 1, (2, 3)))
+V_GROUPS = ((0,), (1,), (2, 3), (4, 5), (6, 7))
 LOADS = (
     ("y", 0, 0, (0,)),
     ("y", 0, 0, (1,)),
@@ -85,18 +87,24 @@ def tile_pinnlayer_pb_kernel(tc, Volt, Y, Yconj, out_0, out_1):
             return raw[:, K * n : K * (n + 1)]
 
         grp = {}
+        for m, h, ts in Y_GROUPS:
+            tile = keep.tile([P, 1024 * len(ts)], BF16, name="ygrp%d%d%d" % (m, h, ts[0]), align_bytes=64)
+            for t in ts:
+                grp[("y", m, h, t)] = (tile, len(ts), t - ts[0])
+        for rows in V_GROUPS:
+            tile = keep.tile([P, 1024 * len(rows)], BF16, name="vgrp%d" % rows[0], align_bytes=64)
+            for i in rows:
+                grp[("v", i)] = (tile, len(rows), i - rows[0])
         codes = {}
         scales = {}
         o_sb = {}
         for m in range(2):
             for h in range(2):
-                grp[(m, h)] = keep.tile([P, 4096], BF16, name="ygrp%d%d" % (m, h), align_bytes=64)
                 codes[(m, h)] = keep.tile([P, 1024], U32, name="ycod%d%d" % (m, h), align_bytes=64)
                 scales[(m, h)] = keep.tile([P, 1024], U8, name="yscl%d%d" % (m, h), align_bytes=64)
             for j in range(4):
                 o_sb[(m, j)] = keep.tile([P, 2048], F32, name="osb%d%d" % (m, j))
         for j in range(4):
-            grp[j] = keep.tile([P, 2048], BF16, name="vgrp%d" % j, align_bytes=64)
             codes[j] = keep.tile([P, 512], U32, name="vcod%d" % j, align_bytes=64)
             scales[j] = keep.tile([P, 512], U8, name="vscl%d" % j, align_bytes=64)
 
@@ -132,27 +140,32 @@ def tile_pinnlayer_pb_kernel(tc, Volt, Y, Yconj, out_0, out_1):
             nc.scalar.copy(out=dest, in_=ps[:].rearrange("p (g u) r -> p g r u", g=2))
 
         def flip_y(m, h, t):
-            dest = grp[(m, h)][:].bitcast(F32).rearrange("p (g t q u) -> p g t q u", g=2, t=4, u=2)[:, :, t, :, :]
+            tile, n, c = grp[("y", m, h, t)]
+            dest = tile[:].bitcast(F32).rearrange("p (g t q u) -> p g t q u", g=2, t=n, u=2)[:, :, c, :, :]
             flip(("y", m, h, t), dest, (m, h) in SORTED_Y)
 
         def flip_v(i):
-            j, c = divmod(i, 2)
-            dest = grp[j][:].bitcast(F32).rearrange("p (c g b u) -> p c g b u", c=2, g=2, u=2)[:, c, :, :, :]
+            tile, n, c = grp[("v", i)]
+            dest = tile[:].bitcast(F32).rearrange("p (c g b u) -> p c g b u", c=n, g=2, u=2)[:, c, :, :, :]
             flip(("v", i), dest, i in SORTED_V)
 
         def quant_y(m, h, *ts):
+            tile, n, c = grp[("y", m, h, ts[0])]
             for g in range(2):
                 lo = 512 * g + P * ts[0]
-                hi = lo + P * len(ts)
+                hi = lo + P * n
                 nc.vector.quantize_mx(
-                    out=codes[(m, h)][:, lo:hi].bitcast(FP8X4), scales=scales[(m, h)][:, lo:hi], in_=grp[(m, h)][:, 4 * lo : 4 * hi]
+                    out=codes[(m, h)][:, lo:hi].bitcast(FP8X4),
+                    scales=scales[(m, h)][:, lo:hi],
+                    in_=tile[:, 512 * n * g : 512 * n * (g + 1)],
                 )
 
         def quant_v(*rows):
+            tile, n, c = grp[("v", rows[0])]
             j, c = divmod(rows[0], 2)
             lo = 256 * c
-            hi = lo + 256 * len(rows)
-            nc.vector.quantize_mx(out=codes[j][:, lo:hi].bitcast(FP8X4), scales=scales[j][:, lo:hi], in_=grp[j][:, 4 * lo : 4 * hi])
+            hi = lo + 256 * n
+            nc.vector.quantize_mx(out=codes[j][:, lo:hi].bitcast(FP8X4), scales=scales[j][:, lo:hi], in_=tile[:])
 
         sums = {}
 

@@ -15,9 +15,7 @@ K = 1024
 KW = K // 2
 FLOPS = 2 * 2 * 1024 * 1024 * 1024
 
-OFFLOAD = ((1, 1, 0), (1, 3, 0), (1, 5, 0), (1, 6, 0))
-SORTED_V = (2, 3, 4, 5, 6, 7)
-SORTED_Y = ((1, 0), (1, 1))
+OFFLOAD = ((1, 1, 0), (1, 4, 0))
 Y_GROUPS = ((0, 0, (0,)), (0, 0, (1,)), (0, 0, (2,)), (0, 0, (3,)), (0, 1, (0,)), (0, 1, (1,)), (0, 1, (2,)), (0, 1, (3,)), (1, 0, (0, 1)), (1, 0, (2, 3)), (1, 1, (0, 1)), (1, 1, (2, 3)))
 V_GROUPS = ((0,), (1,), (2, 3), (4, 5), (6, 7))
 LOADS = (
@@ -60,7 +58,6 @@ def tile_pinnlayer_pb_kernel(tc, Volt, Y, Yconj, out_0, out_1):
                 nc.tensor.matmul(out=w[:], lhsT=zeros[:, 0:P], rhs=zeros[:], start=True, stop=True)
 
         home = {}
-        pieces = {}
         for load in LOADS:
             first = load[-1][0]
             rows = len(load[-1])
@@ -128,11 +125,11 @@ def tile_pinnlayer_pb_kernel(tc, Volt, Y, Yconj, out_0, out_1):
         def sort_v(copy, *rows):
             sort(copy, [("v", i) for i in rows])
 
-        def flip(chunk, dest, in_order):
+        def flip(chunk, dest):
             ps = tp_pool.tile([P, 4, P], F32)
             for w in range(4):
                 g, u = divmod(w, 2)
-                if in_order:
+                if chunk in ordered:
                     piece = ordered[chunk][:, P * w : P * (w + 1)]
                 else:
                     piece = words(chunk)[:, 2 * P * g + u : 2 * P * (g + 1) : 2]
@@ -142,12 +139,12 @@ def tile_pinnlayer_pb_kernel(tc, Volt, Y, Yconj, out_0, out_1):
         def flip_y(m, h, t):
             tile, n, c = grp[("y", m, h, t)]
             dest = tile[:].bitcast(F32).rearrange("p (g t q u) -> p g t q u", g=2, t=n, u=2)[:, :, c, :, :]
-            flip(("y", m, h, t), dest, (m, h) in SORTED_Y)
+            flip(("y", m, h, t), dest)
 
         def flip_v(i):
             tile, n, c = grp[("v", i)]
             dest = tile[:].bitcast(F32).rearrange("p (c g b u) -> p c g b u", c=n, g=2, u=2)[:, c, :, :, :]
-            flip(("v", i), dest, i in SORTED_V)
+            flip(("v", i), dest)
 
         def quant_y(m, h, *ts):
             tile, n, c = grp[("y", m, h, ts[0])]
@@ -222,12 +219,14 @@ def tile_pinnlayer_pb_kernel(tc, Volt, Y, Yconj, out_0, out_1):
         warm(8)
         for t in range(4):
             flip_y(0, 0, t)
+            if t % 2: warm(1)
             quant_y(0, 0, t)
         for i in range(2):
             flip_v(i)
             quant_v(i)
         for t in range(4):
             flip_y(0, 1, t)
+            if t==1: warm(1)
             if t == 2:
                 sort_v(ON_V, 2, 3)
             quant_y(0, 1, t)

@@ -15,7 +15,7 @@ K = 1024
 KW = K // 2
 FLOPS = 2 * 2 * 1024 * 1024 * 1024
 
-OFFLOAD = ((1, 1, 0), (1, 4, 0))
+OFFLOAD = ((1, 1, 0), (1, 2, 0))
 Y_GROUPS = ((0, 0, (0,)), (0, 0, (1,)), (0, 0, (2,)), (0, 0, (3,)), (0, 1, (0,)), (0, 1, (1,)), (0, 1, (2,)), (0, 1, (3,)), (1, 0, (0, 1)), (1, 0, (2, 3)), (1, 1, (0, 1)), (1, 1, (2, 3)))
 V_GROUPS = ((0,), (1,), (2, 3), (4, 5), (6, 7))
 LOADS = (
@@ -43,8 +43,7 @@ def tile_pinnlayer_pb_kernel(tc, Volt, Y, Yconj, out_0, out_1):
 
     with ExitStack() as ctx:
         keep = ctx.enter_context(tc.tile_pool(name="keep", bufs=1))
-        tp_pool = ctx.enter_context(tc.psum_pool(name="tp", bufs=4))
-        acc_pool = ctx.enter_context(tc.psum_pool(name="acc", bufs=4))
+        banks = ctx.enter_context(tc.psum_pool(name="banks", bufs=8))
         ctx.enter_context(tc.manual_schedule())
 
         ident = keep.tile([P, P], F32, name="ident")
@@ -54,7 +53,7 @@ def tile_pinnlayer_pb_kernel(tc, Volt, Y, Yconj, out_0, out_1):
 
         def warm(count):
             for n in range(count):
-                w = acc_pool.tile([P, 512], F32, tag="acc", name="warm")
+                w = banks.tile([P, 512], F32, tag="bank", name="warm")
                 nc.tensor.matmul(out=w[:], lhsT=zeros[:, 0:P], rhs=zeros[:], start=True, stop=True)
 
         home = {}
@@ -126,7 +125,7 @@ def tile_pinnlayer_pb_kernel(tc, Volt, Y, Yconj, out_0, out_1):
             sort(copy, [("v", i) for i in rows])
 
         def flip(chunk, dest):
-            ps = tp_pool.tile([P, 4, P], F32)
+            ps = banks.tile([P, 4, P], F32, tag="bank", name="ps")
             for w in range(4):
                 g, u = divmod(w, 2)
                 if chunk in ordered:
@@ -168,7 +167,7 @@ def tile_pinnlayer_pb_kernel(tc, Volt, Y, Yconj, out_0, out_1):
 
         def mx(m, i, h):
             j, c = divmod(i, 2)
-            acc = acc_pool.tile([P, 512], F32, tag="acc", name="acc")
+            acc = banks.tile([P, 512], F32, tag="bank", name="acc")
             for g in range(2):
                 lo = 256 * c + P * g
                 nc.tensor.matmul_mx(
@@ -255,26 +254,27 @@ def tile_pinnlayer_pb_kernel(tc, Volt, Y, Yconj, out_0, out_1):
         row(0, 3)
         row(0, 4)
         sort_y(ON_S, 1, 1, 0, 1)
+        row(0, 5)
         for t in range(4):
             flip_y(1, 0, t)
         quant_y(1, 0, 0, 1)
         sort_y(ON_S, 1, 1, 2, 3)
-        row(0, 5)
-        quant_y(1, 0, 2, 3)
         row(0, 6)
+        quant_y(1, 0, 2, 3)
+        row(0, 7)
         for t in range(4):
             flip_y(1, 1, t)
-        row(0, 7)
-        quant_y(1, 1, 0, 1)
-        mx(1, 0, 0)
-        mx(1, 1, 0)
-        quant_y(1, 1, 2, 3)
-        product(1, 0, 0)
-        product(1, 1, 0)
-        for i in range(2):
-            mx(1, i, 1)
-            product(1, i, 1)
-            store_rows(1, i)
-        for i in range(2, 7):
+        for i in range(3): mx(1,i,0)
+        for i in range(3):
+            if i==0: quant_y(1,1,0,1)
+            if i==0: quant_y(1,1,2,3)
+            product(1,i,0)
+            if i<1: store_tile(1,i,0)
+        for i in range(3):
+            mx(1,i,1)
+            product(1,i,1)
+            if i<1: store_tile(1,i,1)
+            else: store_rows(1,i)
+        for i in range(3, 7):
             row(1, i)
         row(1, 7, True)

@@ -15,7 +15,7 @@ K = 1024
 KW = K // 2
 FLOPS = 2 * 2 * 1024 * 1024 * 1024
 
-OFFLOAD = ((1, 1, 0), (1, 2, 0))
+OFFLOAD = ((1, 2, 0), (1, 3, 0))
 Y_GROUPS = ((0, 0, (0,)), (0, 0, (1,)), (0, 0, (2,)), (0, 0, (3,)), (0, 1, (0,)), (0, 1, (1,)), (0, 1, (2,)), (0, 1, (3,)), (1, 0, (0, 1)), (1, 0, (2, 3)), (1, 1, (0, 1)), (1, 1, (2, 3)))
 V_GROUPS = ((0,), (1,), (2, 3), (4, 5), (6, 7))
 LOADS = (
@@ -218,14 +218,15 @@ def tile_pinnlayer_pb_kernel(tc, Volt, Y, Yconj, out_0, out_1):
         warm(8)
         for t in range(4):
             flip_y(0, 0, t)
-            if t % 2: warm(1)
+            if t == 1: warm(1)
             quant_y(0, 0, t)
         for i in range(2):
             flip_v(i)
+            if i == 0: warm(1)
             quant_v(i)
         for t in range(4):
             flip_y(0, 1, t)
-            if t==1: warm(1)
+            if t == 1: warm(1)
             if t == 2:
                 sort_v(ON_V, 2, 3)
             quant_y(0, 1, t)
@@ -255,26 +256,26 @@ def tile_pinnlayer_pb_kernel(tc, Volt, Y, Yconj, out_0, out_1):
         row(0, 4)
         sort_y(ON_S, 1, 1, 0, 1)
         row(0, 5)
-        for t in range(4):
-            flip_y(1, 0, t)
+        flip_y(1,0,0); flip_y(1,0,1)
+        flip_y(1,0,2); flip_y(1,0,3)
         quant_y(1, 0, 0, 1)
         sort_y(ON_S, 1, 1, 2, 3)
         row(0, 6)
         quant_y(1, 0, 2, 3)
         row(0, 7)
-        for t in range(4):
-            flip_y(1, 1, t)
-        for i in range(3): mx(1,i,0)
-        for i in range(3):
+        flip_y(1,1,0); flip_y(1,1,1)
+        flip_y(1,1,2); flip_y(1,1,3)
+        for i in range(4): mx(1,i,0)
+        for i in range(4):
             if i==0: quant_y(1,1,0,1)
-            if i==0: quant_y(1,1,2,3)
+            if i==1: quant_y(1,1,2,3)
             product(1,i,0)
-            if i<1: store_tile(1,i,0)
-        for i in range(3):
+            if i<2: store_tile(1,i,0)
+        for i in range(4):
             mx(1,i,1)
             product(1,i,1)
-            if i<1: store_tile(1,i,1)
+            if i<2: store_tile(1,i,1)
             else: store_rows(1,i)
-        for i in range(3, 7):
+        for i in range(4, 7):
             row(1, i)
-        row(1, 7, True)
+        row(1, 7)

from contextlib import ExitStack

import concourse.mybir as mybir
from concourse.masks import make_identity

F32 = mybir.dt.float32
BF16 = mybir.dt.bfloat16
U32 = mybir.dt.uint32
U8 = mybir.dt.uint8
FP8X4 = mybir.dt.float8_e4m3fn_x4
MULT = mybir.AluOpType.mult

P = 128
K = 1024
KW = K // 2
FLOPS = 2 * 2 * 1024 * 1024 * 1024

OFFLOAD = ((1, 2, 0), (1, 3, 0))
Y_GROUPS = ((0, 0, (0,)), (0, 0, (1,)), (0, 0, (2,)), (0, 0, (3,)), (0, 1, (0,)), (0, 1, (1,)), (0, 1, (2,)), (0, 1, (3,)), (1, 0, (0, 1)), (1, 0, (2, 3)), (1, 1, (0, 1)), (1, 1, (2, 3)))
V_GROUPS = ((0,), (1,), (2, 3), (4, 5), (6, 7))
LOADS = (
    ("y", 0, 0, (0,)),
    ("y", 0, 0, (1,)),
    ("y", 0, 0, (2, 3)),
    ("v", (0, 1)),
    ("y", 0, 1, (0, 1)),
    ("y", 0, 1, (2, 3)),
    ("v", (2, 3)),
    ("v", (4, 5)),
    ("v", (6, 7)),
    ("y", 1, 0, (0, 1)),
    ("y", 1, 0, (2, 3)),
    ("y", 1, 1, (0, 1)),
    ("y", 1, 1, (2, 3)),
)


def tile_pinnlayer_pb_kernel(tc, Volt, Y, Yconj, out_0, out_1):
    nc = tc.nc
    mats = (Y, Yconj)
    out_views = tuple(o.rearrange("(p t) r -> p t r", t=8) for o in (out_0, out_1))
    volt_view = Volt.rearrange("(p t) k -> p t k", t=8)

    with ExitStack() as ctx:
        keep = ctx.enter_context(tc.tile_pool(name="keep", bufs=1))
        banks = ctx.enter_context(tc.psum_pool(name="banks", bufs=8))
        ctx.enter_context(tc.manual_schedule())

        ident = keep.tile([P, P], F32, name="ident")
        make_identity(nc, ident[:])
        zeros = keep.tile([P, 512], BF16, name="zeros")
        nc.vector.memset(zeros[:], 0.0)

        def warm(count):
            for n in range(count):
                w = banks.tile([P, 512], F32, tag="bank", name="warm")
                nc.tensor.matmul(out=w[:], lhsT=zeros[:, 0:P], rhs=zeros[:], start=True, stop=True)

        home = {}
        for load in LOADS:
            first = load[-1][0]
            rows = len(load[-1])
            if load[0] == "y":
                m, h = load[1:3]
                view = mats[m][512 * h : 512 * (h + 1), :].rearrange("(q t) k -> q t k", t=4)
                chunks = [("y", m, h, t) for t in load[-1]]
                name = "y%d%d%d" % (m, h, first)
            else:
                view = volt_view
                chunks = [("v", i) for i in load[-1]]
                name = "v%d" % first
            raw = keep.tile([P, rows * K], BF16, name="raw" + name)
            nc.sync.dma_start(out=raw[:].rearrange("p (t k) -> p t k", t=rows), in_=view[:, first : first + rows, :])
            for n in range(rows):
                home[chunks[n]] = (raw, n)

        def words(chunk):
            raw, n = home[chunk]
            return raw[:].bitcast(F32)[:, KW * n : KW * (n + 1)]

        def volt_row(i):
            raw, n = home[("v", i)]
            return raw[:, K * n : K * (n + 1)]

        grp = {}
        for m, h, ts in Y_GROUPS:
            tile = keep.tile([P, 1024 * len(ts)], BF16, name="ygrp%d%d%d" % (m, h, ts[0]), align_bytes=64)
            for t in ts:
                grp[("y", m, h, t)] = (tile, len(ts), t - ts[0])
        for rows in V_GROUPS:
            tile = keep.tile([P, 1024 * len(rows)], BF16, name="vgrp%d" % rows[0], align_bytes=64)
            for i in rows:
                grp[("v", i)] = (tile, len(rows), i - rows[0])
        codes = {}
        scales = {}
        o_sb = {}
        for m in range(2):
            for h in range(2):
                codes[(m, h)] = keep.tile([P, 1024], U32, name="ycod%d%d" % (m, h), align_bytes=64)
                scales[(m, h)] = keep.tile([P, 1024], U8, name="yscl%d%d" % (m, h), align_bytes=64)
            for j in range(4):
                o_sb[(m, j)] = keep.tile([P, 2048], F32, name="osb%d%d" % (m, j))
        for j in range(4):
            codes[j] = keep.tile([P, 512], U32, name="vcod%d" % j, align_bytes=64)
            scales[j] = keep.tile([P, 512], U8, name="vscl%d" % j, align_bytes=64)

        ON_V = nc.vector.tensor_copy
        ON_S = nc.scalar.copy
        ordered = {}

        def sort(copy, chunks):
            raw, n = home[chunks[0]]
            srt = keep.tile([P, KW * len(chunks)], F32, name="srt" + "".join(str(x) for x in chunks[0]))
            copy(
                out=srt[:].rearrange("p (x u q) -> p x u q", u=2, q=P),
                in_=raw[:].bitcast(F32)[:, KW * n : KW * (n + len(chunks))].rearrange("p (x q u) -> p x u q", u=2, q=P),
            )
            for c in range(len(chunks)):
                ordered[chunks[c]] = srt[:, KW * c : KW * (c + 1)]

        def sort_y(copy, m, h, *ts):
            sort(copy, [("y", m, h, t) for t in ts])

        def sort_v(copy, *rows):
            sort(copy, [("v", i) for i in rows])

        def flip(chunk, dest):
            ps = banks.tile([P, 4, P], F32, tag="bank", name="ps")
            for w in range(4):
                g, u = divmod(w, 2)
                if chunk in ordered:
                    piece = ordered[chunk][:, P * w : P * (w + 1)]
                else:
                    piece = words(chunk)[:, 2 * P * g + u : 2 * P * (g + 1) : 2]
                nc.tensor.transpose(ps[:, w, :], piece, ident[:])
            nc.scalar.copy(out=dest, in_=ps[:].rearrange("p (g u) r -> p g r u", g=2))

        def flip_y(m, h, t):
            tile, n, c = grp[("y", m, h, t)]
            dest = tile[:].bitcast(F32).rearrange("p (g t q u) -> p g t q u", g=2, t=n, u=2)[:, :, c, :, :]
            flip(("y", m, h, t), dest)

        def flip_v(i):
            tile, n, c = grp[("v", i)]
            dest = tile[:].bitcast(F32).rearrange("p (c g b u) -> p c g b u", c=n, g=2, u=2)[:, c, :, :, :]
            flip(("v", i), dest)

        def quant_y(m, h, *ts):
            tile, n, c = grp[("y", m, h, ts[0])]
            for g in range(2):
                lo = 512 * g + P * ts[0]
                hi = lo + P * n
                nc.vector.quantize_mx(
                    out=codes[(m, h)][:, lo:hi].bitcast(FP8X4),
                    scales=scales[(m, h)][:, lo:hi],
                    in_=tile[:, 512 * n * g : 512 * n * (g + 1)],
                )

        def quant_v(*rows):
            tile, n, c = grp[("v", rows[0])]
            j, c = divmod(rows[0], 2)
            lo = 256 * c
            hi = lo + 256 * n
            nc.vector.quantize_mx(out=codes[j][:, lo:hi].bitcast(FP8X4), scales=scales[j][:, lo:hi], in_=tile[:])

        sums = {}

        def mx(m, i, h):
            j, c = divmod(i, 2)
            acc = banks.tile([P, 512], F32, tag="bank", name="acc")
            for g in range(2):
                lo = 256 * c + P * g
                nc.tensor.matmul_mx(
                    out=acc[:],
                    lhsT=codes[j][:, lo : lo + P].bitcast(FP8X4),
                    lhsT_scale=scales[j][:, lo : lo + P],
                    rhs=codes[(m, h)][:, 512 * g : 512 * (g + 1)].bitcast(FP8X4),
                    rhs_scale=scales[(m, h)][:, 512 * g : 512 * (g + 1)],
                    start=(g == 0),
                    stop=(g == 1),
                )
            sums[(m, i, h)] = acc

        def product(m, i, h):
            j, c = divmod(i, 2)
            dst = o_sb[(m, j)][:, 1024 * c + 512 * h : 1024 * c + 512 * (h + 1)]
            fac = volt_row(i)[:, 512 * h : 512 * (h + 1)]
            src = sums[(m, i, h)][:].rearrange("b (t q) -> b q t", t=4)
            dst3 = dst.rearrange("b (q t) -> b q t", t=4)
            if (m, i, h) in OFFLOAD:
                nc.scalar.copy(out=dst3, in_=src)
                nc.gpsimd.tensor_tensor(out=dst, in0=dst, in1=fac, op=MULT)
            else:
                nc.vector.tensor_tensor(out=dst3, in0=src, in1=fac.rearrange("b (q t) -> b q t", t=4), op=MULT)

        def store_rows(m, *rows):
            j, c = divmod(rows[0], 2)
            lo = 1024 * c
            hi = lo + 1024 * len(rows)
            nc.sync.dma_start(
                out=out_views[m][:, rows[0] : rows[0] + len(rows), :], in_=o_sb[(m, j)][:, lo:hi].rearrange("p (c r) -> p c r", r=1024)
            )

        def store_tile(m, i, h):
            j, c = divmod(i, 2)
            lo = 1024 * c + 512 * h
            nc.sync.dma_start(out=out_views[m][:, i, 512 * h : 512 * (h + 1)], in_=o_sb[(m, j)][:, lo : lo + 512])

        def row(m, i, split=False):
            for h in range(2):
                mx(m, i, h)
            for h in range(2):
                product(m, i, h)
                if split:
                    store_tile(m, i, h)
            if not split:
                store_rows(m, i)
        warm(8)
        for t in range(4):
            flip_y(0, 0, t)
            if t == 1: warm(1)
            quant_y(0, 0, t)
        for i in range(2):
            flip_v(i)
            if i == 0: warm(1)
            quant_v(i)
        for t in range(4):
            flip_y(0, 1, t)
            if t == 1: warm(1)
            if t == 2:
                sort_v(ON_V, 2, 3)
            quant_y(0, 1, t)
        mx(0, 0, 0)
        mx(0, 1, 0)
        sort_v(ON_V, 4, 5)
        product(0, 0, 0)
        product(0, 1, 0)
        for i in range(2, 6):
            flip_v(i)
        quant_v(2, 3)
        sort_v(ON_V, 6, 7)
        quant_v(4, 5)
        sort_y(ON_S, 1, 0, 0, 1)
        mx(0, 0, 1)
        mx(0, 1, 1)
        product(0, 0, 1)
        store_rows(0, 0)
        product(0, 1, 1)
        store_rows(0, 1)
        row(0, 2)
        flip_v(6)
        flip_v(7)
        quant_v(6, 7)
        sort_y(ON_S, 1, 0, 2, 3)
        row(0, 3)
        row(0, 4)
        sort_y(ON_S, 1, 1, 0, 1)
        row(0, 5)
        flip_y(1,0,0); flip_y(1,0,1)
        flip_y(1,0,2); flip_y(1,0,3)
        quant_y(1, 0, 0, 1)
        sort_y(ON_S, 1, 1, 2, 3)
        row(0, 6)
        quant_y(1, 0, 2, 3)
        row(0, 7)
        flip_y(1,1,0); flip_y(1,1,1)
        flip_y(1,1,2); flip_y(1,1,3)
        for i in range(4): mx(1,i,0)
        for i in range(4):
            if i==0: quant_y(1,1,0,1)
            if i==1: quant_y(1,1,2,3)
            product(1,i,0)
            if i<2: store_tile(1,i,0)
        for i in range(4):
            mx(1,i,1)
            product(1,i,1)
            if i<2: store_tile(1,i,1)
            else: store_rows(1,i)
        for i in range(4, 7):
            row(1, i)
        row(1, 7)
